import numpy as np
import ml_dtypes


def mxq(x, axis, fmt="e4m3"):
    dtype, down = {"e4m3": (ml_dtypes.float8_e4m3fn, 7), "e5m2": (ml_dtypes.float8_e5m2, 14)}[fmt]
    v = np.moveaxis(np.asarray(x, np.float32).astype(ml_dtypes.bfloat16).astype(np.float64), axis, -1)
    blocks = v.reshape(v.shape[:-1] + (-1, 32))
    amax = np.abs(blocks).max(-1, keepdims=True)
    byte = np.maximum(np.where(amax > 0, np.frexp(amax)[1] - 1 + 127, 0) - down, 1)
    scale = np.exp2(byte - 127.0)
    codes = (blocks / scale).astype(np.float32).astype(dtype).astype(np.float64)
    return np.moveaxis((codes * scale).reshape(v.shape), -1, axis)


WIDE = False


def mx_kscale(k):
    if not WIDE:
        return np.ones(k)
    levels = np.array([10, -10, 5, -5, 0])
    if k % 512:
        return np.exp2(np.random.permutation(np.resize(levels, k // 32))).repeat(32)
    a = np.empty((k // 512, 16))
    for p in range(k // 512):
        a[p, :8] = np.random.permutation(np.resize(levels, 8))
        for g in range(8):
            far = levels[np.abs(levels - a[p, g]) >= 10]
            a[p, g + 8] = far[np.random.randint(len(far))]
    return np.exp2(a.ravel()).repeat(32)


BF16 = ml_dtypes.bfloat16


def bf(x):
    return np.asarray(x, np.float32).astype(BF16)


def f64(x):
    return np.asarray(x).astype(np.float64)


B, T, C, H, KH, D = 4, 128, 2048, 16, 4, 128
HD = H * D


def sigmoid(v):
    return 1.0 / (1.0 + np.exp(-v))


def draw0():
    s, t = mx_kscale(C), mx_kscale(HD)
    return {"x": bf(np.random.standard_normal((B, T, C)) * s),
            "y_attn": bf((np.random.standard_normal((B, T, HD)) * 0.3 * t).reshape(B, T, H, D)),
            "w_gate": bf(np.random.standard_normal((C, HD)) / np.sqrt(C) / s[:, None]),
            "w_proj": bf(np.random.standard_normal((HD, C)) * 3.0 / np.sqrt(HD) / t[:, None])}


def core(x, y_attn, w_gate, w_proj):
    gate = sigmoid((mxq(f64(x), 2, "e4m3") @ mxq(f64(w_gate), 0, "e4m3")).reshape(B, T, H, D))
    y = f64(y_attn) * gate
    return mxq(y.reshape(B, T, HD), 2, "e4m3") @ mxq(f64(w_proj), 0, "e4m3")


def e4m3fn_bytes(y):
    return np.clip(np.asarray(y, np.float64), -448.0, 448.0).astype(np.float32).astype(ml_dtypes.float8_e4m3fn).view(np.uint8)


def e4m3fn_values(b):
    return np.asarray(b, np.uint8).view(ml_dtypes.float8_e4m3fn).astype(np.float64)


def setup_inputs():
    d = draw0()
    x0 = np.asarray(d['w_proj']).astype(np.float64)
    s = (np.max(np.abs(x0), axis=(1,), keepdims=True) / 448.0).astype(np.float32)
    out = {}
    for k, v in d.items():
        if k == 'w_proj':
            out['w_proj_bytes'] = e4m3fn_bytes(x0 / s.astype(np.float64))
            out['w_proj_scale'] = s
        else:
            out[k] = v
    return out


def reference(x, y_attn, w_gate, w_proj_bytes, w_proj_scale):
    return core(x, y_attn, w_gate, e4m3fn_values(w_proj_bytes) * w_proj_scale.astype(np.float64))

@@ -1,0 +1,291 @@
+from contextlib import ExitStack
+
+import concourse.mybir as mybir
+from concourse.masks import make_identity
+
+F32 = mybir.dt.float32
+BF16 = mybir.dt.bfloat16
+U32 = mybir.dt.uint32
+U8 = mybir.dt.uint8
+FP8 = mybir.dt.float8_e4m3fn
+FP8X4 = mybir.dt.float8_e4m3fn_x4
+ACT = mybir.ActivationFunctionType
+ALU = mybir.AluOpType
+
+P = 128
+PACK = 4
+B, T, C, HD = 4, 128, 2048, 2048
+TOK = B * T
+KP = P * PACK
+NG = C // KP
+W = 512
+HALF = TOK // 2
+FLOPS = 2 * TOK * C * HD + 2 * TOK * HD * C
+
+ORDER = ([(kd, 0, kk) for kk in range(NG) for kd in ("g", "p")]
+         + [(kd, cc, kk) for kd in ("g", "p") for cc in (1, 2, 3) for kk in range(NG)])
+SCALAR_POS = frozenset((8, 10, 11, 14, 17, 29))
+AHEAD = 7
+D_SIG, D_MUL, D_OUT, D_WID, X_AT = 1, 4, 2, 2, 3
+
+
+def tile_multiheadattention_pb_kernel(tc, x, y_attn, w_gate, w_bytes, w_scale, out):
+    nc = tc.nc
+    with ExitStack() as ctx:
+        const = ctx.enter_context(tc.tile_pool(name="const", bufs=1))
+        io = ctx.enter_context(tc.tile_pool(name="io", bufs=1))
+        work = ctx.enter_context(tc.tile_pool(name="work", bufs=1))
+        codes = ctx.enter_context(tc.tile_pool(name="codes", bufs=1))
+        psum = ctx.enter_context(tc.psum_pool(name="psum", bufs=1))
+
+        ident = const.tile([P, P], F32, name="ident")
+        make_identity(nc, ident[:])
+        warm = const.tile([P, 2], F32, name="warm")
+        nc.vector.memset(warm[:], 0.0)
+        nc.scalar.activation(out=warm[:, 1:2], in_=warm[:, 0:1], func=ACT.Sigmoid)
+        scale = const.tile([P, NG * PACK], F32, name="scale")
+
+        y_view = y_attn.rearrange("b t h d -> t b (h d)")
+
+        def bank_tile(tag="acc", bufs=6):
+            return psum.tile([P, 512], F32, name=tag, tag=tag, bufs=bufs)
+
+        def code_pair(tag, bufs):
+            cd = codes.tile([P, W], U32, name=tag + "_c", tag=tag + "_c", bufs=bufs, align_bytes=64)
+            sc = codes.tile([P, W], U8, name=tag + "_s", tag=tag + "_s", bufs=bufs, align_bytes=64)
+            return cd, sc
+
+        def grp_tile():
+            return work.tile([P, PACK * W], BF16, name="grp", tag="grp", bufs=7, align_bytes=64)
+
+        def quantize(grp, pair):
+            nc.vector.quantize_mx(out=pair[0][:].bitcast(FP8X4), scales=pair[1][:], in_=grp[:])
+
+        raw, ytile, xt, wb, wide, grp, wcode = {}, {}, {}, {}, {}, {}, {}
+        xg, xcode, hg, hcode, gate, ybank = {}, {}, {}, {}, {}, {}
+        acc, acc2 = {}, {}
+
+        def load_gate_unit(i):
+            c, k = divmod(i, NG)
+            t = io.tile([P, PACK, W], BF16, name="raw", tag="raw", bufs=7)
+            nc.sync.dma_start(out=t[:], in_=w_gate[k * KP:(k + 1) * KP, c * W:(c + 1) * W].rearrange("(p j) w -> p j w", j=PACK))
+            raw[i] = t
+
+        def load_x(b):
+            t = io.tile([P, C], BF16, name="xt", tag="xt", bufs=4)
+            nc.sync.dma_start(out=t[:], in_=x[b])
+            xt[b] = t
+
+        def load_y(c):
+            t = io.tile([P, B, W], BF16, name="yt", tag="yt", bufs=2)
+            nc.sync.dma_start(out=t[:], in_=y_view[:, :, c * W:(c + 1) * W])
+            ytile[c] = t
+
+        def load_bytes(j):
+            h, c = divmod(j, NG)
+            t = io.tile([P, PACK, 2 * W], U8, name="wb", tag="wb", bufs=6)
+            nc.sync.dma_start(out=t[:], in_=w_bytes[c * KP:(c + 1) * KP, h * 2 * W:(h + 1) * 2 * W].rearrange("(p j) w -> p j w", j=PACK))
+            wb[h, c] = t
+
+        nb = [0]
+
+        def loads_for(i):
+            load_gate_unit(i)
+            if i == 0:
+                load_x(0)
+                load_x(1)
+            if i == 1:
+                load_x(2)
+                load_x(3)
+            if i >= NG and i % NG == 0:
+                load_y(i // NG - 1)
+            if i >= 3 and i % 2 == 1:
+                if nb[0] == 0:
+                    nc.sync.dma_start(out=scale[:].rearrange("p (c j) -> p c j", j=PACK), in_=w_scale.rearrange("(c p j) o -> p c (j o)", p=P, j=PACK))
+                load_bytes(nb[0])
+                nb[0] += 1
+
+        def transpose_words(words, half, *bank_args):
+            bank = bank_tile(*bank_args)
+            for u in range(2):
+                for r in range(2):
+                    o = u * HALF + r * P
+                    nc.tensor.transpose(bank[:, o:o + P], words(2 * half + r, u), ident[:])
+            return bank
+
+        def x_transpose(g, half):
+            def words(b, u):
+                return xt[b][:].bitcast(F32)[:, g * 256 + u:(g + 1) * 256:2]
+            bank = transpose_words(words, half)
+            if g not in xg:
+                xg[g] = grp_tile()
+            dst = xg[g][:, half * 1024:(half + 1) * 1024].bitcast(F32).rearrange("p (r u) -> p r u", u=2)
+            nc.scalar.copy(out=dst, in_=bank[:].rearrange("p (u r) -> p r u", u=2))
+
+        def x_quantize(g):
+            xcode[g] = code_pair("x", NG)
+            quantize(xg[g], xcode[g])
+
+        def y_transpose(c, half):
+            yw = ytile[c][:].rearrange("p b w -> p (b w)").bitcast(F32)
+
+            def words(b, u):
+                return yw[:, b * 256 + u:(b + 1) * 256:2]
+            ybank[c, half] = transpose_words(words, half, "ytr", 2)
+
+        def widen(j):
+            n, c = divmod(j, NG)
+            h, nn = divmod(n, 2)
+            t = work.tile([P, PACK, W], BF16, name="wide", tag="wide", bufs=5)
+            for q in range(PACK):
+                nc.scalar.activation(out=t[:, q, :], in_=wb[h, c][:, q, nn * W:(nn + 1) * W].bitcast(FP8), func=ACT.Copy,
+                                     scale=scale[:, c * PACK + q:c * PACK + q + 1])
+            wide[j] = t
+
+        def pos_of(i):
+            return ORDER.index(("g", *divmod(i, NG)) if i < NG * NG else ("p", *divmod(i - NG * NG, NG)))
+
+        def interleave(i):
+            g = grp_tile()
+            if i < NG * NG:
+                dst = g[:].rearrange("p (t m j) -> p m j t", t=PACK, j=PACK)
+                src = raw[i][:].rearrange("p j (m t) -> p m j t", t=PACK)
+            else:
+                dst = g[:].rearrange("p (m i t) -> p m t i", i=4, t=PACK)
+                src = wide[i - NG * NG][:].rearrange("p t (m i) -> p m t i", i=4)
+            if pos_of(i) in SCALAR_POS:
+                nc.scalar.copy(out=dst, in_=src)
+            else:
+                nc.vector.tensor_copy(out=dst, in_=src)
+            grp[i] = g
+
+        def unit_quantize(i):
+            wcode[i] = code_pair("w", 8) if i < NG * NG else code_pair("p", 10)
+            quantize(grp[i], wcode[i])
+
+        def stage1(c):
+            for half in range(2):
+                for u in range(2):
+                    bank = bank_tile()
+                    acc[c, half, u] = bank
+                    for e in range(2):
+                        t = 2 * u + e
+                        for k in range(NG):
+                            wc, ws = wcode[c * NG + k]
+                            xc, xs = xcode[k]
+                            nc.tensor.matmul_mx(
+                                out=bank[:, e * HALF:(e + 1) * HALF],
+                                lhsT=wc[:, t * P:(t + 1) * P].bitcast(FP8X4), lhsT_scale=ws[:, t * P:(t + 1) * P],
+                                rhs=xc[:, half * HALF:(half + 1) * HALF].bitcast(FP8X4), rhs_scale=xs[:, half * HALF:(half + 1) * HALF],
+                                start=(k == 0), stop=(k == NG - 1))
+
+        def sigmoid(c, half):
+            s = work.tile([P, 2, HALF, 2], F32, name="gate", tag="gate", bufs=4)
+            for u in range(2):
+                nc.scalar.activation(out=s[:, u, :, :], in_=acc[c, half, u][:].rearrange("p (e n) -> p n e", e=2), func=ACT.Sigmoid)
+            gate[c, half] = s
+
+        def multiply(c, half):
+            if c not in hg:
+                hg[c] = grp_tile()
+            dst = hg[c][:, half * 1024:(half + 1) * 1024].rearrange("p (n u e) -> p n u e", u=2, e=2)
+            nc.vector.tensor_tensor(
+                out=dst, in0=gate[c, half][:].rearrange("p u n e -> p n u e"),
+                in1=ybank[c, half][:].bitcast(BF16).rearrange("p (u n e) -> p n u e", u=2, e=2), op=ALU.mult)
+
+        def h_quantize(c):
+            hcode[c] = code_pair("h", NG)
+            quantize(hg[c], hcode[c])
+
+        def stage2(n, c):
+            wc, ws = wcode[NG * NG + n * NG + c]
+            hc, hs = hcode[c]
+            for b in range(B):
+                if c == 0:
+                    acc2[n, b] = bank_tile()
+                nc.tensor.matmul_mx(
+                    out=acc2[n, b][:], lhsT=hc[:, b * P:(b + 1) * P].bitcast(FP8X4), lhsT_scale=hs[:, b * P:(b + 1) * P],
+                    rhs=wc[:].bitcast(FP8X4), rhs_scale=ws[:], start=(c == 0), stop=(c == NG - 1))
+
+        def drain_out(n, b):
+            r = io.tile([P, W], F32, name="res", tag="res", bufs=8)
+            if b % 2 == 0:
+                nc.scalar.copy(out=r[:], in_=acc2[n, b][:])
+            else:
+                nc.vector.tensor_copy(out=r[:], in_=acc2[n, b][:])
+            nc.sync.dma_start(out=out[b][:, n * W:(n + 1) * W], in_=r[:])
+
+        wb_next = [0]
+
+        def load_for(pos):
+            kind, a, b = ORDER[pos]
+            if kind == "g":
+                load_gate_unit(a * NG + b)
+                if b == 0 and a > 0:
+                    load_y(a - 1)
+                if a == NG - 1 and b == NG - 1:
+                    load_y(a)
+            elif a % 2 == 0:
+                load_bytes((a // 2) * NG + b)
+            if a == 0 and kind == "p":
+                load_x(b)
+
+        def index(pos):
+            kind, a, b = ORDER[pos]
+            return a * NG + b + (NG * NG if kind == "p" else 0)
+
+        for pos in range(AHEAD):
+            load_for(pos)
+            if pos == 0:
+                nc.sync.dma_start(out=scale[:].rearrange("p (c j) -> p c j", j=PACK), in_=w_scale.rearrange("(c p j) o -> p c (j o)", p=P, j=PACK))
+        h_at = [None] * NG
+        sched = {}
+
+        def at(step, fn, *args):
+            sched.setdefault(step, []).append((fn, args))
+
+        for g in range(NG):
+            at(X_AT, x_transpose, g, 0)
+        for g in range(NG):
+            at(X_AT + 1, x_transpose, g, 1)
+        for g in range(NG):
+            at(X_AT + 2 + g // 2, x_quantize, g)
+        last_h = 0
+        for pos, (kind, a, b) in enumerate(ORDER):
+            if kind == "g" and b == NG - 1:
+                q = pos + 1
+                at(q, y_transpose, a, 0)
+                at(q, y_transpose, a, 1)
+                at(q, stage1, a)
+                at(q + D_SIG, sigmoid, a, 0)
+                at(q + D_SIG + 1, sigmoid, a, 1)
+                at(q + D_MUL, multiply, a, 0)
+                at(q + D_MUL + 1, multiply, a, 1)
+                at(q + D_MUL + 2, h_quantize, a)
+                last_h = q + D_MUL + 2
+        prev = 0
+        for n in range(NG):
+            for c in range(NG):
+                q = max(ORDER.index(("p", n, c)) + 1, last_h, prev)
+                prev = q
+                at(q, stage2, n, c)
+            for b in range(B):
+                at(min(prev + D_OUT, len(ORDER) + 1), drain_out, n, b)
+        p_list = [pos for pos, o in enumerate(ORDER) if o[0] == "p"]
+        widened = 0
+        for i in range(max(sched) + 1):
+            if i + AHEAD < len(ORDER):
+                load_for(i + AHEAD)
+            while widened < len(p_list) and p_list[widened] <= i + (0 if i == 0 else D_WID):
+                widen(index(p_list[widened]) - NG * NG)
+                widened += 1
+                if i > 0 and p_list[widened - 1] > i:
+                    break
+            if i + 1 < len(ORDER) and i + 1 in SCALAR_POS:
+                interleave(index(i + 1))
+            if i < len(ORDER) and i not in SCALAR_POS:
+                interleave(index(i))
+            if 1 <= i <= len(ORDER):
+                unit_quantize(index(i - 1))
+            for fn, args in sched.get(i, []):
+                fn(*args)

@@ -148,8 +148,8 @@ def tile_multiheadattention_pb_kernel(tc, x, y_attn, w_gate, w_bytes, w_scale, o
         def interleave(i):
             g = grp_tile()
             if i < NG * NG:
-                dst = g[:].rearrange("p (t m j) -> p m j t", t=PACK, j=PACK)
-                src = raw[i][:].rearrange("p j (m t) -> p m j t", t=PACK)
+                dst = g[:].rearrange("p (t m i j) -> p m t i j", t=PACK, i=2, j=PACK)
+                src = raw[i][:].rearrange("p j (m i t) -> p m t i j", i=2, t=PACK)
             else:
                 dst = g[:].rearrange("p (m i t) -> p m t i", i=4, t=PACK)
                 src = wide[i - NG * NG][:].rearrange("p t (m i) -> p m t i", i=4)

@@ -16,17 +16,36 @@ P = 128
 PACK = 4
 B, T, C, HD = 4, 128, 2048, 2048
 TOK = B * T
-KP = P * PACK
-NG = C // KP
+K_PASS = P * PACK
+PASSES = C // K_PASS
 W = 512
 HALF = TOK // 2
+GATE_UNITS = PASSES * PASSES
+LAST_UNIT = 2 * GATE_UNITS - 1
+LAST_N = HD // W - 1
+HALF_W = W // 2
 FLOPS = 2 * TOK * C * HD + 2 * TOK * HD * C
 
-ORDER = ([(kd, 0, kk) for kk in range(NG) for kd in ("g", "p")]
-         + [(kd, cc, kk) for kd in ("g", "p") for cc in (1, 2, 3) for kk in range(NG)])
-SCALAR_POS = frozenset((8, 10, 11, 14, 17, 29))
-AHEAD = 7
-D_SIG, D_MUL, D_OUT, D_WID, X_AT = 1, 4, 2, 2, 3
+LAST_VECTOR_GROUPS = 88
+
+ORDER = """
+lb.1.0 ls lb.1.1 lb.1.2 lb.1.3 wi.5.V wi.1.S lb.3 il.17.S il.21.V wi.7.V lb.0 lx.2 lg.4 lx.3 lx.0 lx.1 wi.4.V
+il.23.S il.20.S il.4.S lg.6 wi.3.V qu.21 wi.0.V tx.2.1 qu.17 il.16.V il.19.V qu.23 tx.2.0 tx.3.1 tx.3.0 lb.2
+lg.7 lg.5 lg.0 cx.2.1.V il.6.S cx.3.0.S cx.2.0.S tx.1.0 tx.0.0 tx.1.1 qu.20 qu.19 qu.16 qu.4 wi.6.V il.5.V
+cx.1.0.S cx.3.1.S lg.2 tx.0.1 il.7.S lg.15 cx.0.0.S cx.1.1.S cx.0.1.S qx.3 lg.3 qu.6 qx.2 qu.5 il.22.V qx.1 qx.0
+qu.7 il.2.V qu.22 il.0.S lg.13 lg.1 il.1.V il.13.V qu.1 qu.2 il.3.S qu.3 mg.1.0.1 mg.1.1.1 mg.1.1.0 mg.1.0.0
+lg.11 lb.4 lg.12 lg.14 il.15.S ly.1 sg.1.0.1 wi.12.S sg.1.1.1 il.12.V qu.0 mg.0.1.0 mg.0.1.1 lg.9 lg.10 sg.1.0.0
+sg.1.1.0 lg.8 wi.2.S ty.1.0 ly.0 lb.7 lb.5 lb.6 ly.2 mg.0.0.0 qu.12 sg.0.1.1 il.14.V qu.13 mg.0.0.1 il.9.V
+sg.0.1.0 qu.14 il.18.S il.11.S il.10.V qu.15 mg.3.0.1 il.8.V mg.3.1.1 ty.1.1 mu.1.0 qu.10 qu.9 mu.1.1 mg.3.1.0
+mg.3.0.0 ty.0.0 ty.0.1 sg.3.0.1 qu.8 qu.11 sg.0.0.0 sg.0.0.1 sg.3.1.0 il.28.S sg.3.1.1 mg.2.0.1 qh.1 mu.0.0
+mu.0.1 mg.2.1.0 ly.3 ty.3.0 ty.3.1 mg.2.0.0 sg.3.0.0 wi.8.V qu.18 mu.3.0 mu.3.1 qh.0 wi.11.V mg.2.1.1 wi.15.S
+sg.2.1.0 sg.2.1.1 sg.2.0.1 sg.2.0.0 ty.2.1 ty.2.0 mu.2.1 wi.10.S wi.9.S mu.2.0 qh.3 qh.2 il.26.V mo.0.0 mo.0.1
+mo.0.3 mo.0.2 st.0.0.S il.24.V st.0.1.S wi.13.V il.25.S st.0.3.S st.0.2.S qu.28 qu.24 qu.26 il.27.V qu.25 mo.1.2
+mo.1.3 mo.1.0 mo.1.1 st.1.0.S st.1.1.S mo.2.0 il.31 st.1.3.V qu.27 mo.2.1 mo.2.2 st.1.2.S wi.14.V qu.31.0
+qu.31.1 il.29.S qu.29 mo.2.3 mo.3.0.1 st.2.0.S il.30.V mo.3.3.1 st.2.2.S st.2.1.S st.2.3.S qu.30 mo.3.1.1
+mo.3.3.0 mo.3.1.0 mo.3.2.1 mo.3.2.0 mo.3.0.0 sp.0.1.V sp.1.1.V sp.3.1.S sp.2.1.S sp.0.0.S sp.3.0.S sp.1.0.V
+sp.2.0.S
+"""
 
 
 def tile_multiheadattention_pb_kernel(tc, x, y_attn, w_gate, w_bytes, w_scale, out):
@@ -43,249 +62,201 @@ def tile_multiheadattention_pb_kernel(tc, x, y_attn, w_gate, w_bytes, w_scale, o
         warm = const.tile([P, 2], F32, name="warm")
         nc.vector.memset(warm[:], 0.0)
         nc.scalar.activation(out=warm[:, 1:2], in_=warm[:, 0:1], func=ACT.Sigmoid)
-        scale = const.tile([P, NG * PACK], F32, name="scale")
+        scale = const.tile([P, PASSES * PACK], F32, name="scale")
+
+        ctx.enter_context(tc.manual_schedule())
 
         y_view = y_attn.rearrange("b t h d -> t b (h d)")
 
-        def bank_tile(tag="acc", bufs=6):
-            return psum.tile([P, 512], F32, name=tag, tag=tag, bufs=bufs)
+        raw, x_rows, y_rows, byte_rows = {}, {}, {}, {}
+        widened, grouped, unit_codes = {}, {}, {}
+        x_bank, x_grouped, x_codes = {}, {}, {}
+        y_bank, gate_bank, gate, h_grouped, h_codes = {}, {}, {}, {}, {}
+        out_bank, passes_done, result = {}, {}, {}
 
-        def code_pair(tag, bufs):
-            cd = codes.tile([P, W], U32, name=tag + "_c", tag=tag + "_c", bufs=bufs, align_bytes=64)
-            sc = codes.tile([P, W], U8, name=tag + "_s", tag=tag + "_s", bufs=bufs, align_bytes=64)
-            return cd, sc
+        def main_bank():
+            return psum.tile([P, 512], F32, name="main", tag="main", bufs=6)
 
-        def grp_tile():
+        def side_bank():
+            return psum.tile([P, 512], F32, name="side", tag="side", bufs=2)
+
+        def code_tiles(tag, bufs):
+            words = codes.tile([P, W], U32, name=tag + "_words", tag=tag + "_words", bufs=bufs, align_bytes=64)
+            scales = codes.tile([P, W], U8, name=tag + "_scales", tag=tag + "_scales", bufs=bufs, align_bytes=64)
+            return words, scales
+
+        def group_tile():
             return work.tile([P, PACK * W], BF16, name="grp", tag="grp", bufs=7, align_bytes=64)
 
-        def quantize(grp, pair):
-            nc.vector.quantize_mx(out=pair[0][:].bitcast(FP8X4), scales=pair[1][:], in_=grp[:])
+        def quantize(words, scales, values):
+            nc.vector.quantize_mx(out=words.bitcast(FP8X4), scales=scales, in_=values)
 
-        raw, ytile, xt, wb, wide, grp, wcode = {}, {}, {}, {}, {}, {}, {}
-        xg, xcode, hg, hcode, gate, ybank = {}, {}, {}, {}, {}, {}
-        acc, acc2 = {}, {}
-
-        def load_gate_unit(i):
-            c, k = divmod(i, NG)
-            t = io.tile([P, PACK, W], BF16, name="raw", tag="raw", bufs=7)
-            nc.sync.dma_start(out=t[:], in_=w_gate[k * KP:(k + 1) * KP, c * W:(c + 1) * W].rearrange("(p j) w -> p j w", j=PACK))
-            raw[i] = t
-
-        def load_x(b):
-            t = io.tile([P, C], BF16, name="xt", tag="xt", bufs=4)
-            nc.sync.dma_start(out=t[:], in_=x[b])
-            xt[b] = t
-
-        def load_y(c):
-            t = io.tile([P, B, W], BF16, name="yt", tag="yt", bufs=2)
-            nc.sync.dma_start(out=t[:], in_=y_view[:, :, c * W:(c + 1) * W])
-            ytile[c] = t
-
-        def load_bytes(j):
-            h, c = divmod(j, NG)
-            t = io.tile([P, PACK, 2 * W], U8, name="wb", tag="wb", bufs=6)
-            nc.sync.dma_start(out=t[:], in_=w_bytes[c * KP:(c + 1) * KP, h * 2 * W:(h + 1) * 2 * W].rearrange("(p j) w -> p j w", j=PACK))
-            wb[h, c] = t
-
-        nb = [0]
-
-        def loads_for(i):
-            load_gate_unit(i)
-            if i == 0:
-                load_x(0)
-                load_x(1)
-            if i == 1:
-                load_x(2)
-                load_x(3)
-            if i >= NG and i % NG == 0:
-                load_y(i // NG - 1)
-            if i >= 3 and i % 2 == 1:
-                if nb[0] == 0:
-                    nc.sync.dma_start(out=scale[:].rearrange("p (c j) -> p c j", j=PACK), in_=w_scale.rearrange("(c p j) o -> p c (j o)", p=P, j=PACK))
-                load_bytes(nb[0])
-                nb[0] += 1
-
-        def transpose_words(words, half, *bank_args):
-            bank = bank_tile(*bank_args)
-            for u in range(2):
-                for r in range(2):
-                    o = u * HALF + r * P
-                    nc.tensor.transpose(bank[:, o:o + P], words(2 * half + r, u), ident[:])
-            return bank
-
-        def x_transpose(g, half):
-            def words(b, u):
-                return xt[b][:].bitcast(F32)[:, g * 256 + u:(g + 1) * 256:2]
-            bank = transpose_words(words, half)
-            if g not in xg:
-                xg[g] = grp_tile()
-            dst = xg[g][:, half * 1024:(half + 1) * 1024].bitcast(F32).rearrange("p (r u) -> p r u", u=2)
-            nc.scalar.copy(out=dst, in_=bank[:].rearrange("p (u r) -> p r u", u=2))
-
-        def x_quantize(g):
-            xcode[g] = code_pair("x", NG)
-            quantize(xg[g], xcode[g])
-
-        def y_transpose(c, half):
-            yw = ytile[c][:].rearrange("p b w -> p (b w)").bitcast(F32)
-
-            def words(b, u):
-                return yw[:, b * 256 + u:(b + 1) * 256:2]
-            ybank[c, half] = transpose_words(words, half, "ytr", 2)
-
-        def widen(j):
-            n, c = divmod(j, NG)
-            h, nn = divmod(n, 2)
-            t = work.tile([P, PACK, W], BF16, name="wide", tag="wide", bufs=5)
-            for q in range(PACK):
-                nc.scalar.activation(out=t[:, q, :], in_=wb[h, c][:, q, nn * W:(nn + 1) * W].bitcast(FP8), func=ACT.Copy,
-                                     scale=scale[:, c * PACK + q:c * PACK + q + 1])
-            wide[j] = t
-
-        def pos_of(i):
-            return ORDER.index(("g", *divmod(i, NG)) if i < NG * NG else ("p", *divmod(i - NG * NG, NG)))
-
-        def interleave(i):
-            g = grp_tile()
-            if i < NG * NG:
-                dst = g[:].rearrange("p (t m i j) -> p m t i j", t=PACK, i=2, j=PACK)
-                src = raw[i][:].rearrange("p j (m i t) -> p m t i j", i=2, t=PACK)
-            else:
-                dst = g[:].rearrange("p (m i t) -> p m t i", i=4, t=PACK)
-                src = wide[i - NG * NG][:].rearrange("p t (m i) -> p m t i", i=4)
-            if pos_of(i) in SCALAR_POS:
+        def copy(engine, dst, src):
+            if engine == "S":
                 nc.scalar.copy(out=dst, in_=src)
             else:
                 nc.vector.tensor_copy(out=dst, in_=src)
-            grp[i] = g
 
-        def unit_quantize(i):
-            wcode[i] = code_pair("w", 8) if i < NG * NG else code_pair("p", 10)
-            quantize(grp[i], wcode[i])
+        def load_scale():
+            nc.sync.dma_start(out=scale[:].rearrange("p (c t) -> p c t", t=PACK),
+                              in_=w_scale.rearrange("(c p t) o -> p c (t o)", p=P, t=PACK))
 
-        def stage1(c):
-            for half in range(2):
-                for u in range(2):
-                    bank = bank_tile()
-                    acc[c, half, u] = bank
-                    for e in range(2):
-                        t = 2 * u + e
-                        for k in range(NG):
-                            wc, ws = wcode[c * NG + k]
-                            xc, xs = xcode[k]
-                            nc.tensor.matmul_mx(
-                                out=bank[:, e * HALF:(e + 1) * HALF],
-                                lhsT=wc[:, t * P:(t + 1) * P].bitcast(FP8X4), lhsT_scale=ws[:, t * P:(t + 1) * P],
-                                rhs=xc[:, half * HALF:(half + 1) * HALF].bitcast(FP8X4), rhs_scale=xs[:, half * HALF:(half + 1) * HALF],
-                                start=(k == 0), stop=(k == NG - 1))
+        def load_gate(unit):
+            c, k = divmod(unit, PASSES)
+            raw[unit] = io.tile([P, PACK, W], BF16, name="raw", tag="raw", bufs=7)
+            rows = w_gate[k * K_PASS:(k + 1) * K_PASS, c * W:(c + 1) * W]
+            nc.sync.dma_start(out=raw[unit][:], in_=rows.rearrange("(p j) w -> p j w", j=PACK))
 
-        def sigmoid(c, half):
-            s = work.tile([P, 2, HALF, 2], F32, name="gate", tag="gate", bufs=4)
+        def load_x(b):
+            x_rows[b] = io.tile([P, C], BF16, name="x_rows", tag="rows", bufs=4)
+            nc.sync.dma_start(out=x_rows[b][:], in_=x[b])
+
+        def load_y(c):
+            y_rows[c] = io.tile([P, B, W], BF16, name="y_rows", tag="rows", bufs=4)
+            nc.sync.dma_start(out=y_rows[c][:], in_=y_view[:, :, c * W:(c + 1) * W])
+
+        def load_bytes(pair, t=None):
+            h, c = divmod(pair, PASSES)
+            if (h, c) not in byte_rows:
+                byte_rows[h, c] = io.tile([P, PACK, 2 * W], U8, name="byte_rows", tag="byte_rows", bufs=6)
+            dst = byte_rows[h, c][:]
+            src = w_bytes[c * K_PASS:(c + 1) * K_PASS, h * 2 * W:(h + 1) * 2 * W].rearrange("(p j) w -> p j w", j=PACK)
+            if t is None:
+                nc.sync.dma_start(out=dst, in_=src)
+            else:
+                nc.sync.dma_start(out=dst[:, t, :], in_=src[:, t, :])
+
+        def transpose_words(bank, half, words):
             for u in range(2):
-                nc.scalar.activation(out=s[:, u, :, :], in_=acc[c, half, u][:].rearrange("p (e n) -> p n e", e=2), func=ACT.Sigmoid)
-            gate[c, half] = s
+                for r in range(2):
+                    start = u * HALF + r * P
+                    nc.tensor.transpose(bank[:, start:start + P], words(2 * half + r, u), ident[:])
+
+        def transpose_x(k, half):
+            def words(b, u):
+                return x_rows[b][:].bitcast(F32)[:, k * 256 + u:(k + 1) * 256:2]
+            x_bank[k, half] = main_bank()
+            transpose_words(x_bank[k, half], half, words)
+
+        def copy_x(k, half, engine):
+            if k not in x_grouped:
+                x_grouped[k] = group_tile()
+            dst = x_grouped[k][:, half * 1024:(half + 1) * 1024].bitcast(F32).rearrange("p (r u) -> p r u", u=2)
+            copy(engine, dst, x_bank[k, half][:].rearrange("p (u r) -> p r u", u=2))
+
+        def quantize_x(k):
+            x_codes[k] = code_tiles("x", PASSES)
+            quantize(x_codes[k][0][:], x_codes[k][1][:], x_grouped[k][:])
+
+        def transpose_y(c, half):
+            all_words = y_rows[c][:].rearrange("p b w -> p (b w)").bitcast(F32)
+
+            def words(b, u):
+                return all_words[:, b * 256 + u:(b + 1) * 256:2]
+            y_bank[c, half] = side_bank()
+            transpose_words(y_bank[c, half], half, words)
+
+        def widen(j, engine):
+            n, c = divmod(j, PASSES)
+            h, side = divmod(n, 2)
+            widened[j] = work.tile([P, PACK, W], BF16, name="wide", tag="wide", bufs=5)
+            for t in range(PACK):
+                src = byte_rows[h, c][:, t, side * W:(side + 1) * W].bitcast(FP8)
+                factor = scale[:, c * PACK + t:c * PACK + t + 1]
+                if engine == "S":
+                    nc.scalar.activation(out=widened[j][:, t, :], in_=src, func=ACT.Copy, scale=factor)
+                else:
+                    nc.vector.tensor_scalar(out=widened[j][:, t, :], in0=src, scalar1=factor, scalar2=None, op0=ALU.mult)
+
+        def interleave(unit, engine=None):
+            grouped[unit] = group_tile()
+            if unit < GATE_UNITS:
+                dst = grouped[unit][:].rearrange("p (t m j) -> p m j t", t=PACK, j=PACK)
+                src = raw[unit][:].rearrange("p j (m t) -> p m j t", t=PACK)
+            else:
+                dst = grouped[unit][:].rearrange("p (m i t) -> p m t i", i=4, t=PACK)
+                src = widened[unit - GATE_UNITS][:].rearrange("p t (m i) -> p m t i", i=4)
+            if unit == LAST_UNIT:
+                nc.vector.tensor_copy(out=dst[:, :LAST_VECTOR_GROUPS], in_=src[:, :LAST_VECTOR_GROUPS])
+                nc.scalar.copy(out=dst[:, LAST_VECTOR_GROUPS:], in_=src[:, LAST_VECTOR_GROUPS:])
+            else:
+                copy(engine, dst, src)
+
+        def quantize_unit(unit, part=None):
+            if unit not in unit_codes:
+                unit_codes[unit] = code_tiles("gate", 8) if unit < GATE_UNITS else code_tiles("proj", GATE_UNITS)
+            words, scales = unit_codes[unit]
+            cols = slice(0, W) if part is None else slice(part * HALF_W, (part + 1) * HALF_W)
+            quantize(words[:, cols], scales[:, cols], grouped[unit][:, PACK * cols.start:PACK * cols.stop])
+
+        def matmul_gate(c, half, u):
+            gate_bank[c, half, u] = main_bank()
+            tokens = slice(half * HALF, (half + 1) * HALF)
+            for e in range(2):
+                chans = slice((2 * u + e) * P, (2 * u + e + 1) * P)
+                for k in range(PASSES):
+                    w_words, w_scales = unit_codes[c * PASSES + k]
+                    x_words, x_scales = x_codes[k]
+                    nc.tensor.matmul_mx(
+                        out=gate_bank[c, half, u][:, e * HALF:(e + 1) * HALF],
+                        lhsT=w_words[:, chans].bitcast(FP8X4), lhsT_scale=w_scales[:, chans],
+                        rhs=x_words[:, tokens].bitcast(FP8X4), rhs_scale=x_scales[:, tokens],
+                        start=(k == 0), stop=(k == PASSES - 1))
+
+        def sigmoid(c, half, u):
+            if (c, half) not in gate:
+                gate[c, half] = work.tile([P, 2, HALF, 2], F32, name="gate", tag="gate", bufs=4)
+            nc.scalar.activation(out=gate[c, half][:, u, :, :], in_=gate_bank[c, half, u][:].rearrange("p (e n) -> p n e", e=2),
+                                 func=ACT.Sigmoid)
 
         def multiply(c, half):
-            if c not in hg:
-                hg[c] = grp_tile()
-            dst = hg[c][:, half * 1024:(half + 1) * 1024].rearrange("p (n u e) -> p n u e", u=2, e=2)
+            if c not in h_grouped:
+                h_grouped[c] = group_tile()
+            dst = h_grouped[c][:, half * 1024:(half + 1) * 1024].rearrange("p (n u e) -> p n u e", u=2, e=2)
             nc.vector.tensor_tensor(
                 out=dst, in0=gate[c, half][:].rearrange("p u n e -> p n u e"),
-                in1=ybank[c, half][:].bitcast(BF16).rearrange("p (u n e) -> p n u e", u=2, e=2), op=ALU.mult)
+                in1=y_bank[c, half][:].bitcast(BF16).rearrange("p (u n e) -> p n u e", u=2, e=2), op=ALU.mult)
 
-        def h_quantize(c):
-            hcode[c] = code_pair("h", NG)
-            quantize(hg[c], hcode[c])
+        def quantize_h(c):
+            h_codes[c] = code_tiles("h", PASSES)
+            quantize(h_codes[c][0][:], h_codes[c][1][:], h_grouped[c][:])
 
-        def stage2(n, c):
-            wc, ws = wcode[NG * NG + n * NG + c]
-            hc, hs = hcode[c]
+        def matmul_out(n, c, part=None):
+            w_words, w_scales = unit_codes[GATE_UNITS + n * PASSES + c]
+            h_words, h_scales = h_codes[c]
+            done = passes_done.get((n, part), 0)
+            passes_done[n, part] = done + 1
+            cols = slice(0, W) if part is None else slice(part * HALF_W, (part + 1) * HALF_W)
             for b in range(B):
-                if c == 0:
-                    acc2[n, b] = bank_tile()
+                if done == 0:
+                    out_bank[n, b, part] = side_bank() if part == 1 and b >= 2 else main_bank()
+                toks = slice(b * P, (b + 1) * P)
                 nc.tensor.matmul_mx(
-                    out=acc2[n, b][:], lhsT=hc[:, b * P:(b + 1) * P].bitcast(FP8X4), lhsT_scale=hs[:, b * P:(b + 1) * P],
-                    rhs=wc[:].bitcast(FP8X4), rhs_scale=ws[:], start=(c == 0), stop=(c == NG - 1))
+                    out=out_bank[n, b, part][:, :cols.stop - cols.start],
+                    lhsT=h_words[:, toks].bitcast(FP8X4), lhsT_scale=h_scales[:, toks],
+                    rhs=w_words[:, cols].bitcast(FP8X4), rhs_scale=w_scales[:, cols],
+                    start=(done == 0), stop=(done == PASSES - 1))
 
-        def drain_out(n, b):
-            r = io.tile([P, W], F32, name="res", tag="res", bufs=8)
-            if b % 2 == 0:
-                nc.scalar.copy(out=r[:], in_=acc2[n, b][:])
-            else:
-                nc.vector.tensor_copy(out=r[:], in_=acc2[n, b][:])
-            nc.sync.dma_start(out=out[b][:, n * W:(n + 1) * W], in_=r[:])
+        def store(n, b, part, engine):
+            if (n, b) not in result:
+                result[n, b] = io.tile([P, W], F32, name="result", tag="result", bufs=6)
+            cols = slice(0, W) if part is None else slice(part * HALF_W, (part + 1) * HALF_W)
+            copy(engine, result[n, b][:, cols], out_bank[n, b, part][:, :cols.stop - cols.start])
+            nc.sync.dma_start(out=out[b][:, n * W + cols.start:n * W + cols.stop], in_=result[n, b][:, cols])
 
-        wb_next = [0]
+        def store_chunk(n, b, engine):
+            store(n, b, None, engine)
 
-        def load_for(pos):
-            kind, a, b = ORDER[pos]
-            if kind == "g":
-                load_gate_unit(a * NG + b)
-                if b == 0 and a > 0:
-                    load_y(a - 1)
-                if a == NG - 1 and b == NG - 1:
-                    load_y(a)
-            elif a % 2 == 0:
-                load_bytes((a // 2) * NG + b)
-            if a == 0 and kind == "p":
-                load_x(b)
+        def store_part(b, part, engine):
+            store(LAST_N, b, part, engine)
 
-        def index(pos):
-            kind, a, b = ORDER[pos]
-            return a * NG + b + (NG * NG if kind == "p" else 0)
-
-        for pos in range(AHEAD):
-            load_for(pos)
-            if pos == 0:
-                nc.sync.dma_start(out=scale[:].rearrange("p (c j) -> p c j", j=PACK), in_=w_scale.rearrange("(c p j) o -> p c (j o)", p=P, j=PACK))
-        h_at = [None] * NG
-        sched = {}
-
-        def at(step, fn, *args):
-            sched.setdefault(step, []).append((fn, args))
-
-        for g in range(NG):
-            at(X_AT, x_transpose, g, 0)
-        for g in range(NG):
-            at(X_AT + 1, x_transpose, g, 1)
-        for g in range(NG):
-            at(X_AT + 2 + g // 2, x_quantize, g)
-        last_h = 0
-        for pos, (kind, a, b) in enumerate(ORDER):
-            if kind == "g" and b == NG - 1:
-                q = pos + 1
-                at(q, y_transpose, a, 0)
-                at(q, y_transpose, a, 1)
-                at(q, stage1, a)
-                at(q + D_SIG, sigmoid, a, 0)
-                at(q + D_SIG + 1, sigmoid, a, 1)
-                at(q + D_MUL, multiply, a, 0)
-                at(q + D_MUL + 1, multiply, a, 1)
-                at(q + D_MUL + 2, h_quantize, a)
-                last_h = q + D_MUL + 2
-        prev = 0
-        for n in range(NG):
-            for c in range(NG):
-                q = max(ORDER.index(("p", n, c)) + 1, last_h, prev)
-                prev = q
-                at(q, stage2, n, c)
-            for b in range(B):
-                at(min(prev + D_OUT, len(ORDER) + 1), drain_out, n, b)
-        p_list = [pos for pos, o in enumerate(ORDER) if o[0] == "p"]
-        widened = 0
-        for i in range(max(sched) + 1):
-            if i + AHEAD < len(ORDER):
-                load_for(i + AHEAD)
-            while widened < len(p_list) and p_list[widened] <= i + (0 if i == 0 else D_WID):
-                widen(index(p_list[widened]) - NG * NG)
-                widened += 1
-                if i > 0 and p_list[widened - 1] > i:
-                    break
-            if i + 1 < len(ORDER) and i + 1 in SCALAR_POS:
-                interleave(index(i + 1))
-            if i < len(ORDER) and i not in SCALAR_POS:
-                interleave(index(i))
-            if 1 <= i <= len(ORDER):
-                unit_quantize(index(i - 1))
-            for fn, args in sched.get(i, []):
-                fn(*args)
+        STEPS = {
+            "ls": load_scale, "lg": load_gate, "lx": load_x, "ly": load_y, "lb": load_bytes,
+            "tx": transpose_x, "cx": copy_x, "qx": quantize_x, "ty": transpose_y,
+            "wi": widen, "il": interleave, "qu": quantize_unit,
+            "mg": matmul_gate, "sg": sigmoid, "mu": multiply, "qh": quantize_h,
+            "mo": matmul_out, "st": store_chunk, "sp": store_part,
+        }
+        for step in ORDER.split():
+            parts = step.split(".")
+            STEPS[parts[0]](*[a if a in ("V", "S") else int(a) for a in parts[1:]])

from contextlib import ExitStack

import concourse.mybir as mybir
from concourse.masks import make_identity

F32 = mybir.dt.float32
BF16 = mybir.dt.bfloat16
U32 = mybir.dt.uint32
U8 = mybir.dt.uint8
FP8 = mybir.dt.float8_e4m3fn
FP8X4 = mybir.dt.float8_e4m3fn_x4
ACT = mybir.ActivationFunctionType
ALU = mybir.AluOpType

P = 128
PACK = 4
B, T, C, HD = 4, 128, 2048, 2048
TOK = B * T
K_PASS = P * PACK
PASSES = C // K_PASS
W = 512
HALF = TOK // 2
GATE_UNITS = PASSES * PASSES
LAST_UNIT = 2 * GATE_UNITS - 1
LAST_N = HD // W - 1
HALF_W = W // 2
FLOPS = 2 * TOK * C * HD + 2 * TOK * HD * C

LAST_VECTOR_GROUPS = 88

ORDER = """
lb.1.0 ls lb.1.1 lb.1.2 lb.1.3 wi.5.V wi.1.S lb.3 il.17.S il.21.V wi.7.V lb.0 lx.2 lg.4 lx.3 lx.0 lx.1 wi.4.V
il.23.S il.20.S il.4.S lg.6 wi.3.V qu.21 wi.0.V tx.2.1 qu.17 il.16.V il.19.V qu.23 tx.2.0 tx.3.1 tx.3.0 lb.2
lg.7 lg.5 lg.0 cx.2.1.V il.6.S cx.3.0.S cx.2.0.S tx.1.0 tx.0.0 tx.1.1 qu.20 qu.19 qu.16 qu.4 wi.6.V il.5.V
cx.1.0.S cx.3.1.S lg.2 tx.0.1 il.7.S lg.15 cx.0.0.S cx.1.1.S cx.0.1.S qx.3 lg.3 qu.6 qx.2 qu.5 il.22.V qx.1 qx.0
qu.7 il.2.V qu.22 il.0.S lg.13 lg.1 il.1.V il.13.V qu.1 qu.2 il.3.S qu.3 mg.1.0.1 mg.1.1.1 mg.1.1.0 mg.1.0.0
lg.11 lb.4 lg.12 lg.14 il.15.S ly.1 sg.1.0.1 wi.12.S sg.1.1.1 il.12.V qu.0 mg.0.1.0 mg.0.1.1 lg.9 lg.10 sg.1.0.0
sg.1.1.0 lg.8 wi.2.S ty.1.0 ly.0 lb.7 lb.5 lb.6 ly.2 mg.0.0.0 qu.12 sg.0.1.1 il.14.V qu.13 mg.0.0.1 il.9.V
sg.0.1.0 qu.14 il.18.S il.11.S il.10.V qu.15 mg.3.0.1 il.8.V mg.3.1.1 ty.1.1 mu.1.0 qu.10 qu.9 mu.1.1 mg.3.1.0
mg.3.0.0 ty.0.0 ty.0.1 sg.3.0.1 qu.8 qu.11 sg.0.0.0 sg.0.0.1 sg.3.1.0 il.28.S sg.3.1.1 mg.2.0.1 qh.1 mu.0.0
mu.0.1 mg.2.1.0 ly.3 ty.3.0 ty.3.1 mg.2.0.0 sg.3.0.0 wi.8.V qu.18 mu.3.0 mu.3.1 qh.0 wi.11.V mg.2.1.1 wi.15.S
sg.2.1.0 sg.2.1.1 sg.2.0.1 sg.2.0.0 ty.2.1 ty.2.0 mu.2.1 wi.10.S wi.9.S mu.2.0 qh.3 qh.2 il.26.V mo.0.0 mo.0.1
mo.0.3 mo.0.2 st.0.0.S il.24.V st.0.1.S wi.13.V il.25.S st.0.3.S st.0.2.S qu.28 qu.24 qu.26 il.27.V qu.25 mo.1.2
mo.1.3 mo.1.0 mo.1.1 st.1.0.S st.1.1.S mo.2.0 il.31 st.1.3.V qu.27 mo.2.1 mo.2.2 st.1.2.S wi.14.V qu.31.0
qu.31.1 il.29.S qu.29 mo.2.3 mo.3.0.1 st.2.0.S il.30.V mo.3.3.1 st.2.2.S st.2.1.S st.2.3.S qu.30 mo.3.1.1
mo.3.3.0 mo.3.1.0 mo.3.2.1 mo.3.2.0 mo.3.0.0 sp.0.1.V sp.1.1.V sp.3.1.S sp.2.1.S sp.0.0.S sp.3.0.S sp.1.0.V
sp.2.0.S
"""


def tile_multiheadattention_pb_kernel(tc, x, y_attn, w_gate, w_bytes, w_scale, out):
    nc = tc.nc
    with ExitStack() as ctx:
        const = ctx.enter_context(tc.tile_pool(name="const", bufs=1))
        io = ctx.enter_context(tc.tile_pool(name="io", bufs=1))
        work = ctx.enter_context(tc.tile_pool(name="work", bufs=1))
        codes = ctx.enter_context(tc.tile_pool(name="codes", bufs=1))
        psum = ctx.enter_context(tc.psum_pool(name="psum", bufs=1))

        ident = const.tile([P, P], F32, name="ident")
        make_identity(nc, ident[:])
        warm = const.tile([P, 2], F32, name="warm")
        nc.vector.memset(warm[:], 0.0)
        nc.scalar.activation(out=warm[:, 1:2], in_=warm[:, 0:1], func=ACT.Sigmoid)
        scale = const.tile([P, PASSES * PACK], F32, name="scale")

        ctx.enter_context(tc.manual_schedule())

        y_view = y_attn.rearrange("b t h d -> t b (h d)")

        raw, x_rows, y_rows, byte_rows = {}, {}, {}, {}
        widened, grouped, unit_codes = {}, {}, {}
        x_bank, x_grouped, x_codes = {}, {}, {}
        y_bank, gate_bank, gate, h_grouped, h_codes = {}, {}, {}, {}, {}
        out_bank, passes_done, result = {}, {}, {}

        def main_bank():
            return psum.tile([P, 512], F32, name="main", tag="main", bufs=6)

        def side_bank():
            return psum.tile([P, 512], F32, name="side", tag="side", bufs=2)

        def code_tiles(tag, bufs):
            words = codes.tile([P, W], U32, name=tag + "_words", tag=tag + "_words", bufs=bufs, align_bytes=64)
            scales = codes.tile([P, W], U8, name=tag + "_scales", tag=tag + "_scales", bufs=bufs, align_bytes=64)
            return words, scales

        def group_tile():
            return work.tile([P, PACK * W], BF16, name="grp", tag="grp", bufs=7, align_bytes=64)

        def quantize(words, scales, values):
            nc.vector.quantize_mx(out=words.bitcast(FP8X4), scales=scales, in_=values)

        def copy(engine, dst, src):
            if engine == "S":
                nc.scalar.copy(out=dst, in_=src)
            else:
                nc.vector.tensor_copy(out=dst, in_=src)

        def load_scale():
            nc.sync.dma_start(out=scale[:].rearrange("p (c t) -> p c t", t=PACK),
                              in_=w_scale.rearrange("(c p t) o -> p c (t o)", p=P, t=PACK))

        def load_gate(unit):
            c, k = divmod(unit, PASSES)
            raw[unit] = io.tile([P, PACK, W], BF16, name="raw", tag="raw", bufs=7)
            rows = w_gate[k * K_PASS:(k + 1) * K_PASS, c * W:(c + 1) * W]
            nc.sync.dma_start(out=raw[unit][:], in_=rows.rearrange("(p j) w -> p j w", j=PACK))

        def load_x(b):
            x_rows[b] = io.tile([P, C], BF16, name="x_rows", tag="rows", bufs=4)
            nc.sync.dma_start(out=x_rows[b][:], in_=x[b])

        def load_y(c):
            y_rows[c] = io.tile([P, B, W], BF16, name="y_rows", tag="rows", bufs=4)
            nc.sync.dma_start(out=y_rows[c][:], in_=y_view[:, :, c * W:(c + 1) * W])

        def load_bytes(pair, t=None):
            h, c = divmod(pair, PASSES)
            if (h, c) not in byte_rows:
                byte_rows[h, c] = io.tile([P, PACK, 2 * W], U8, name="byte_rows", tag="byte_rows", bufs=6)
            dst = byte_rows[h, c][:]
            src = w_bytes[c * K_PASS:(c + 1) * K_PASS, h * 2 * W:(h + 1) * 2 * W].rearrange("(p j) w -> p j w", j=PACK)
            if t is None:
                nc.sync.dma_start(out=dst, in_=src)
            else:
                nc.sync.dma_start(out=dst[:, t, :], in_=src[:, t, :])

        def transpose_words(bank, half, words):
            for u in range(2):
                for r in range(2):
                    start = u * HALF + r * P
                    nc.tensor.transpose(bank[:, start:start + P], words(2 * half + r, u), ident[:])

        def transpose_x(k, half):
            def words(b, u):
                return x_rows[b][:].bitcast(F32)[:, k * 256 + u:(k + 1) * 256:2]
            x_bank[k, half] = main_bank()
            transpose_words(x_bank[k, half], half, words)

        def copy_x(k, half, engine):
            if k not in x_grouped:
                x_grouped[k] = group_tile()
            dst = x_grouped[k][:, half * 1024:(half + 1) * 1024].bitcast(F32).rearrange("p (r u) -> p r u", u=2)
            copy(engine, dst, x_bank[k, half][:].rearrange("p (u r) -> p r u", u=2))

        def quantize_x(k):
            x_codes[k] = code_tiles("x", PASSES)
            quantize(x_codes[k][0][:], x_codes[k][1][:], x_grouped[k][:])

        def transpose_y(c, half):
            all_words = y_rows[c][:].rearrange("p b w -> p (b w)").bitcast(F32)

            def words(b, u):
                return all_words[:, b * 256 + u:(b + 1) * 256:2]
            y_bank[c, half] = side_bank()
            transpose_words(y_bank[c, half], half, words)

        def widen(j, engine):
            n, c = divmod(j, PASSES)
            h, side = divmod(n, 2)
            widened[j] = work.tile([P, PACK, W], BF16, name="wide", tag="wide", bufs=5)
            for t in range(PACK):
                src = byte_rows[h, c][:, t, side * W:(side + 1) * W].bitcast(FP8)
                factor = scale[:, c * PACK + t:c * PACK + t + 1]
                if engine == "S":
                    nc.scalar.activation(out=widened[j][:, t, :], in_=src, func=ACT.Copy, scale=factor)
                else:
                    nc.vector.tensor_scalar(out=widened[j][:, t, :], in0=src, scalar1=factor, scalar2=None, op0=ALU.mult)

        def interleave(unit, engine=None):
            grouped[unit] = group_tile()
            if unit < GATE_UNITS:
                dst = grouped[unit][:].rearrange("p (t m j) -> p m j t", t=PACK, j=PACK)
                src = raw[unit][:].rearrange("p j (m t) -> p m j t", t=PACK)
            else:
                dst = grouped[unit][:].rearrange("p (m i t) -> p m t i", i=4, t=PACK)
                src = widened[unit - GATE_UNITS][:].rearrange("p t (m i) -> p m t i", i=4)
            if unit == LAST_UNIT:
                nc.vector.tensor_copy(out=dst[:, :LAST_VECTOR_GROUPS], in_=src[:, :LAST_VECTOR_GROUPS])
                nc.scalar.copy(out=dst[:, LAST_VECTOR_GROUPS:], in_=src[:, LAST_VECTOR_GROUPS:])
            else:
                copy(engine, dst, src)

        def quantize_unit(unit, part=None):
            if unit not in unit_codes:
                unit_codes[unit] = code_tiles("gate", 8) if unit < GATE_UNITS else code_tiles("proj", GATE_UNITS)
            words, scales = unit_codes[unit]
            cols = slice(0, W) if part is None else slice(part * HALF_W, (part + 1) * HALF_W)
            quantize(words[:, cols], scales[:, cols], grouped[unit][:, PACK * cols.start:PACK * cols.stop])

        def matmul_gate(c, half, u):
            gate_bank[c, half, u] = main_bank()
            tokens = slice(half * HALF, (half + 1) * HALF)
            for e in range(2):
                chans = slice((2 * u + e) * P, (2 * u + e + 1) * P)
                for k in range(PASSES):
                    w_words, w_scales = unit_codes[c * PASSES + k]
                    x_words, x_scales = x_codes[k]
                    nc.tensor.matmul_mx(
                        out=gate_bank[c, half, u][:, e * HALF:(e + 1) * HALF],
                        lhsT=w_words[:, chans].bitcast(FP8X4), lhsT_scale=w_scales[:, chans],
                        rhs=x_words[:, tokens].bitcast(FP8X4), rhs_scale=x_scales[:, tokens],
                        start=(k == 0), stop=(k == PASSES - 1))

        def sigmoid(c, half, u):
            if (c, half) not in gate:
                gate[c, half] = work.tile([P, 2, HALF, 2], F32, name="gate", tag="gate", bufs=4)
            nc.scalar.activation(out=gate[c, half][:, u, :, :], in_=gate_bank[c, half, u][:].rearrange("p (e n) -> p n e", e=2),
                                 func=ACT.Sigmoid)

        def multiply(c, half):
            if c not in h_grouped:
                h_grouped[c] = group_tile()
            dst = h_grouped[c][:, half * 1024:(half + 1) * 1024].rearrange("p (n u e) -> p n u e", u=2, e=2)
            nc.vector.tensor_tensor(
                out=dst, in0=gate[c, half][:].rearrange("p u n e -> p n u e"),
                in1=y_bank[c, half][:].bitcast(BF16).rearrange("p (u n e) -> p n u e", u=2, e=2), op=ALU.mult)

        def quantize_h(c):
            h_codes[c] = code_tiles("h", PASSES)
            quantize(h_codes[c][0][:], h_codes[c][1][:], h_grouped[c][:])

        def matmul_out(n, c, part=None):
            w_words, w_scales = unit_codes[GATE_UNITS + n * PASSES + c]
            h_words, h_scales = h_codes[c]
            done = passes_done.get((n, part), 0)
            passes_done[n, part] = done + 1
            cols = slice(0, W) if part is None else slice(part * HALF_W, (part + 1) * HALF_W)
            for b in range(B):
                if done == 0:
                    out_bank[n, b, part] = side_bank() if part == 1 and b >= 2 else main_bank()
                toks = slice(b * P, (b + 1) * P)
                nc.tensor.matmul_mx(
                    out=out_bank[n, b, part][:, :cols.stop - cols.start],
                    lhsT=h_words[:, toks].bitcast(FP8X4), lhsT_scale=h_scales[:, toks],
                    rhs=w_words[:, cols].bitcast(FP8X4), rhs_scale=w_scales[:, cols],
                    start=(done == 0), stop=(done == PASSES - 1))

        def store(n, b, part, engine):
            if (n, b) not in result:
                result[n, b] = io.tile([P, W], F32, name="result", tag="result", bufs=6)
            cols = slice(0, W) if part is None else slice(part * HALF_W, (part + 1) * HALF_W)
            copy(engine, result[n, b][:, cols], out_bank[n, b, part][:, :cols.stop - cols.start])
            nc.sync.dma_start(out=out[b][:, n * W + cols.start:n * W + cols.stop], in_=result[n, b][:, cols])

        def store_chunk(n, b, engine):
            store(n, b, None, engine)

        def store_part(b, part, engine):
            store(LAST_N, b, part, engine)

        STEPS = {
            "ls": load_scale, "lg": load_gate, "lx": load_x, "ly": load_y, "lb": load_bytes,
            "tx": transpose_x, "cx": copy_x, "qx": quantize_x, "ty": transpose_y,
            "wi": widen, "il": interleave, "qu": quantize_unit,
            "mg": matmul_gate, "sg": sigmoid, "mu": multiply, "qh": quantize_h,
            "mo": matmul_out, "st": store_chunk, "sp": store_part,
        }
        for step in ORDER.split():
            parts = step.split(".")
            STEPS[parts[0]](*[a if a in ("V", "S") else int(a) for a in parts[1:]])
